import numpy as np
import ml_dtypes


def mxq(x, axis, fmt="e4m3"):
    dtype, down = {"e4m3": (ml_dtypes.float8_e4m3fn, 7), "e5m2": (ml_dtypes.float8_e5m2, 14)}[fmt]
    v = np.moveaxis(np.asarray(x, np.float32).astype(ml_dtypes.bfloat16).astype(np.float64), axis, -1)
    blocks = v.reshape(v.shape[:-1] + (-1, 32))
    amax = np.abs(blocks).max(-1, keepdims=True)
    byte = np.maximum(np.where(amax > 0, np.frexp(amax)[1] - 1 + 127, 0) - down, 1)
    scale = np.exp2(byte - 127.0)
    codes = (blocks / scale).astype(np.float32).astype(dtype).astype(np.float64)
    return np.moveaxis((codes * scale).reshape(v.shape), -1, axis)


WIDE = False


def mx_kscale(k):
    if not WIDE:
        return np.ones(k)
    levels = np.array([10, -10, 5, -5, 0])
    a = np.random.permutation(np.resize(levels, k // 512 * 4)).reshape(k // 512, 4)
    idx = np.arange(k)
    return np.exp2(a[idx // 512, idx % 128 // 32])


BF16 = ml_dtypes.bfloat16


def bf(x):
    return np.asarray(x, np.float32).astype(BF16)


def f64(x):
    return np.asarray(x).astype(np.float64)


B, T, KA, KT, DIM, NH, HD, E = 16, 512, 256, 256, 512, 8, 128, 8
EPS = 1e-5


def setup_inputs():
    r = np.random.standard_normal
    s = mx_kscale(DIM)
    t = mx_kscale(DIM)
    return {"h_attn": bf(r((B, T, DIM)) * 0.4 * s),
            "x": bf(r((B, T, DIM))),
            "W_o": bf(r((DIM, DIM)) * 2.0 / np.sqrt(DIM) / s[None, :]),
            "b_o": bf(r(DIM) * 0.3 + 0.2),
            "W_ffn": bf(r((DIM, DIM)) / np.sqrt(DIM) / t[None, :]),
            "b_ffn": bf(r(DIM) * 0.3),
            "gamma": bf((1.0 + 0.1 * r(DIM)) * t),
            "beta": bf(0.2 * r(DIM) * t)}


def reference(h_attn, x, W_o, b_o, W_ffn, b_ffn, gamma, beta):
    y = (mxq(f64(h_attn), 2, "e4m3") @ mxq(f64(W_o), 1, "e4m3").T) + f64(b_o) + f64(x)
    mu = y.mean(-1, keepdims=True)
    var = ((y - mu) ** 2).mean(-1, keepdims=True)
    xn = (y - mu) / np.sqrt(var + EPS) * f64(gamma) + f64(beta)
    return np.maximum((mxq(xn, 2, "e4m3") @ mxq(f64(W_ffn), 1, "e4m3").T) + f64(b_ffn), 0.0)

@@ -1,0 +1,268 @@
+from contextlib import ExitStack
+
+import concourse.mybir as mybir
+from concourse.masks import make_identity
+
+F32 = mybir.dt.float32
+BF16 = mybir.dt.bfloat16
+U32 = mybir.dt.uint32
+U8 = mybir.dt.uint8
+FP8X4 = mybir.dt.float8_e4m3fn_x4
+ALU = mybir.AluOpType
+ACT = mybir.ActivationFunctionType
+
+P = 128
+DIM = 512
+TOKENS = 16 * 512
+CH = 8
+NCH = TOKENS // (P * CH)
+NPAIR = TOKENS // (2 * P)
+EPS = 1e-5
+FLOPS = 2 * 2 * TOKENS * DIM * DIM
+
+MANUAL = True
+XP_ENGINE = "G"
+E_ENGINE = "V"
+RELU_ENGINE = "G"
+BIG = 3.0e38
+
+
+def tile_l1regressionmoeactionhead_pc_t_kernel(tc, h_attn, x, W_o, b_o, W_ffn, b_ffn, gamma, beta, out):
+    nc = tc.nc
+    hv = h_attn.flatten_outer_dims().rearrange("(c p j) k -> c p j k", p=P, j=CH)
+    xv = x.flatten_outer_dims().rearrange("(c p j) k -> c p j k", p=P, j=CH)
+    ov = out.flatten_outer_dims().rearrange("(c p j) k -> c p j k", p=P, j=CH)
+
+    with ExitStack() as ctx:
+        const = ctx.enter_context(tc.tile_pool(name="const", bufs=1))
+        loads = ctx.enter_context(tc.tile_pool(name="loads", bufs=4))
+        work = ctx.enter_context(tc.tile_pool(name="work", bufs=2))
+        stats = ctx.enter_context(tc.tile_pool(name="stats", bufs=4))
+        psum = ctx.enter_context(tc.psum_pool(name="psum", bufs=2))
+        if MANUAL:
+            ctx.enter_context(tc.manual_schedule())
+
+        h_tiles = {}
+        x_tiles = {}
+
+        def load_h(c, pieces):
+            h_sb = loads.tile([P, CH, DIM], BF16, tag="h", name="h_sb")
+            h_tiles[c] = h_sb
+            step = CH // pieces
+            for i in range(pieces):
+                nc.sync.dma_start(out=h_sb[:, i * step:(i + 1) * step, :], in_=hv[c][:, i * step:(i + 1) * step, :])
+
+        def load_x(c, pieces):
+            x_sb = loads.tile([P, CH, DIM], BF16, tag="x", name="x_sb")
+            x_tiles[c] = x_sb
+            step = CH // pieces
+            for i in range(pieces):
+                nc.sync.dma_start(out=x_sb[:, i * step:(i + 1) * step, :], in_=xv[c][:, i * step:(i + 1) * step, :])
+
+        wo_sb = const.tile([P, 4, DIM], BF16)
+        nc.sync.dma_start(out=wo_sb[:], in_=W_o.rearrange("(r p) k -> p r k", p=P))
+        load_h(0, 4)
+        bo_b = const.tile([P, DIM], BF16)
+        nc.scalar.dma_start(out=bo_b[:], in_=b_o.partition_broadcast(P))
+        gbr = const.tile([P, P], BF16)
+        nc.vector.memset(gbr[:], 0.0)
+        nc.scalar.dma_start(out=gbr[0:4, :], in_=gamma.rearrange("(t p) -> t p", p=P))
+        nc.scalar.dma_start(out=gbr[4:8, :], in_=beta.rearrange("(t p) -> t p", p=P))
+        load_x(0, 4)
+        wf_sb = const.tile([P, 4, DIM], BF16)
+        nc.sync.dma_start(out=wf_sb[:], in_=W_ffn.rearrange("(r p) k -> p r k", p=P))
+        bf_b = const.tile([P, DIM], BF16)
+        nc.scalar.dma_start(out=bf_b[:], in_=b_ffn.partition_broadcast(P))
+        load_h(1, 1)
+        load_x(1, 1)
+        load_h(2, 1)
+        load_x(2, 1)
+
+        ident_f = const.tile([P, P], F32)
+        make_identity(nc, ident_f[:])
+        ident_b = const.tile([P, P], BF16)
+        make_identity(nc, ident_b[:])
+        eps_t = const.tile([P, 1], F32)
+        nc.vector.memset(eps_t[:], EPS)
+        warm = const.tile([P, 1], F32)
+        nc.scalar.activation(out=warm[:], in_=eps_t[:], func=ACT.Sqrt)
+
+        wog = const.tile([P, DIM * 4], BF16, align_bytes=64)
+        woc = const.tile([P, DIM], U32, align_bytes=64)
+        wos = const.tile([P, DIM], U8, align_bytes=64)
+        wog_w = wog[:].bitcast(F32).rearrange("p (r c u) -> p r c u", r=4, u=2)
+        for half in range(2):
+            wt = psum.tile([P, 2, 2, P], F32, tag="ht", name="wt")
+            for rr in range(2):
+                for u in range(2):
+                    nc.tensor.transpose(wt[:, rr, u, :], wo_sb[:, 2 * half + rr, :].bitcast(F32)[:, u * P:(u + 1) * P], ident_f[:])
+            nc.vector.tensor_copy(out=wog_w[:, 2 * half:2 * half + 2, :, :], in_=wt[:].rearrange("p j u r -> p j r u"))
+        nc.vector.quantize_mx(out=woc[:].bitcast(FP8X4), scales=wos[:], in_=wog[:])
+
+        gb_ps = psum.tile([P, P], BF16, tag="zt", name="gb_ps")
+        nc.tensor.transpose(gb_ps[:], gbr[:], ident_b[:])
+        gb = const.tile([P, 8], F32)
+        nc.vector.tensor_copy(out=gb[:], in_=gb_ps[:, 0:8])
+
+        wfg = const.tile([P, DIM, 4], BF16, align_bytes=64)
+        wfc = const.tile([P, DIM], U32, align_bytes=64)
+        wfs = const.tile([P, DIM], U8, align_bytes=64)
+        for r in range(4):
+            wt2 = psum.tile([P, 4, P], BF16, tag="p2", name="wt2")
+            for t in range(4):
+                nc.tensor.transpose(wt2[:, t, :], wf_sb[:, r, t * P:(t + 1) * P], ident_b[:])
+            nc.scalar.copy(out=wfg[:, r * P:(r + 1) * P, :], in_=wt2[:].rearrange("p t c -> p c t"))
+        nc.vector.quantize_mx(out=wfc[:].bitcast(FP8X4), scales=wfs[:], in_=wfg[:].rearrange("p c t -> p (c t)"))
+
+        S = {}
+
+        def src(tiles, pr, jj):
+            return tiles[pr // 4][:, (pr % 4) * 2 + jj, :]
+
+        def st_xp(pr):
+            xp = work.tile([P, 2, DIM], F32, tag="xp", bufs=4, name="xp")
+            j0 = (pr % 4) * 2
+            eng = nc.gpsimd if XP_ENGINE == "G" else nc.vector
+            eng.tensor_tensor(out=xp[:], in0=x_tiles[pr // 4][:, j0:j0 + 2, :], in1=bo_b[:].unsqueeze(1).to_broadcast([P, 2, DIM]), op=ALU.add)
+            for jj in range(2):
+                S[("xp", pr, jj)] = xp[:, jj, :]
+
+        def st_th(pr):
+            ht = psum.tile([P, 2, 2, P], F32, tag="ht", name="ht")
+            S[("ht", pr)] = ht
+            for jj in range(2):
+                for u in range(2):
+                    nc.tensor.transpose(ht[:, jj, u, :], src(h_tiles, pr, jj).bitcast(F32)[:, u * P:(u + 1) * P], ident_f[:])
+
+        def st_a(pr):
+            hg = work.tile([P, 2 * DIM], BF16, tag="hg", align_bytes=64, name="hg")
+            S[("hg", pr)] = hg
+            nc.scalar.copy(out=hg[:].bitcast(F32).rearrange("p (j r u) -> p j r u", j=2, u=2),
+                           in_=S[("ht", pr)][:].rearrange("p j u r -> p j r u"))
+
+        def st_qh(pr):
+            hc = work.tile([P, 2 * P], U32, tag="hc", bufs=3, align_bytes=64, name="hc")
+            hs = work.tile([P, 2 * P], U8, tag="hs", bufs=3, align_bytes=64, name="hs")
+            S[("hc", pr)] = (hc, hs)
+            nc.vector.quantize_mx(out=hc[:].bitcast(FP8X4), scales=hs[:], in_=S[("hg", pr)][:])
+
+        def st_mx1(pr):
+            hc, hs = S[("hc", pr)]
+            for jj in range(2):
+                p1 = psum.tile([P, DIM], F32, tag="p1", name="p1")
+                S[("p1", pr, jj)] = p1
+                nc.tensor.matmul_mx(out=p1[:], lhsT=hc[:, jj * P:(jj + 1) * P].bitcast(FP8X4), lhsT_scale=hs[:, jj * P:(jj + 1) * P],
+                                    rhs=woc[:].bitcast(FP8X4), rhs_scale=wos[:], start=True, stop=True)
+
+        def st_c(pr):
+            sums = stats.tile([P, 2], F32, tag="sums", name="sums")
+            for jj in range(2):
+                y = work.tile([P, DIM], F32, tag="y", bufs=8, name="y")
+                S[("y", pr, jj)] = y
+                nc.vector.scalar_tensor_tensor(out=y[:], in0=S[("p1", pr, jj)][:], scalar=0.0, in1=S[("xp", pr, jj)],
+                                               op0=ALU.add, op1=ALU.add, accum_out=sums[:, jj:jj + 1])
+            negmu = stats.tile([P, 2], F32, tag="negmu", name="negmu")
+            S[("negmu", pr)] = negmu
+            nc.vector.tensor_scalar(out=negmu[:], in0=sums[:], scalar1=-1.0 / DIM, scalar2=None, op0=ALU.mult)
+
+        def st_d(pr):
+            ssq = stats.tile([P, 2], F32, tag="ssq", name="ssq")
+            negmu = S[("negmu", pr)]
+            for jj in range(2):
+                junk = work.tile([P, DIM], BF16, tag="junk", name="junk")
+                nc.scalar.activation(out=junk[:], in_=S[("y", pr, jj)][:], func=ACT.Square, bias=negmu[:, jj:jj + 1], scale=1.0,
+                                     accum_out=ssq[:, jj:jj + 1])
+            std = stats.tile([P, 2], F32, tag="std", name="std")
+            S[("std", pr)] = std
+            nc.scalar.activation(out=std[:], in_=ssq[:], func=ACT.Sqrt, bias=eps_t[:, 0:1], scale=1.0 / DIM)
+
+        def st_e(pr):
+            rstd = stats.tile([P, 2], F32, tag="rstd", name="rstd")
+            nc.vector.reciprocal(out=rstd[:], in_=S[("std", pr)][:])
+            negmu = S[("negmu", pr)]
+            for jj in range(2):
+                y = S[("y", pr, jj)]
+                eng = nc.vector if E_ENGINE == "V" else nc.gpsimd
+                eng.tensor_scalar(out=y[:], in0=y[:], scalar1=negmu[:, jj:jj + 1], scalar2=rstd[:, jj:jj + 1], op0=ALU.add, op1=ALU.mult)
+
+        def st_tz(pr):
+            for b in range(2):
+                zt = psum.tile([P, 2, 2, P], F32, tag="zt", name="zt")
+                S[("zt", pr, b)] = zt
+                for tt in range(2):
+                    t = 2 * b + tt
+                    for jj in range(2):
+                        nc.tensor.transpose(zt[:, tt, jj, :], S[("y", pr, jj)][:, t * P:(t + 1) * P], ident_f[:])
+
+        def st_f(pr):
+            planes = work.tile([P, 4, 2 * P], BF16, tag="planes", name="planes")
+            S[("planes", pr)] = planes
+            for b in range(2):
+                for tt in range(2):
+                    t = 2 * b + tt
+                    nc.scalar.activation(out=planes[:, t, :], in_=S[("zt", pr, b)][:, tt, :, :].rearrange("p j r -> p (j r)"),
+                                         func=ACT.Identity, bias=gb[:, 4 + t:5 + t], scale=gb[:, t:t + 1])
+
+        def st_f2(pr):
+            xg = work.tile([P, 2 * P, 4], BF16, tag="xg", align_bytes=64, name="xg")
+            S[("xg", pr)] = xg
+            nc.vector.tensor_copy(out=xg[:].rearrange("p (c i) t -> p c t i", i=4),
+                                  in_=S[("planes", pr)][:].rearrange("p t (c i) -> p c t i", i=4))
+
+        def st_qx(pr):
+            xc = work.tile([P, 2 * P], U32, tag="xc", bufs=3, align_bytes=64, name="xc")
+            xs = work.tile([P, 2 * P], U8, tag="xs", bufs=3, align_bytes=64, name="xs")
+            S[("xc", pr)] = (xc, xs)
+            nc.vector.quantize_mx(out=xc[:].bitcast(FP8X4), scales=xs[:], in_=S[("xg", pr)][:].rearrange("p c t -> p (c t)"))
+
+        def st_mx2(pr):
+            xc, xs = S[("xc", pr)]
+            for jj in range(2):
+                p2 = psum.tile([P, DIM], F32, tag="p2", name="p2")
+                S[("p2", pr, jj)] = p2
+                nc.tensor.matmul_mx(out=p2[:], lhsT=xc[:, jj * P:(jj + 1) * P].bitcast(FP8X4), lhsT_scale=xs[:, jj * P:(jj + 1) * P],
+                                    rhs=wfc[:].bitcast(FP8X4), rhs_scale=wfs[:], start=True, stop=True)
+
+        def st_h1(pr):
+            o = work.tile([P, 2, DIM], F32, tag="o", bufs=4, name="o")
+            S[("o", pr)] = o
+            for jj in range(2):
+                nc.vector.tensor_tensor(out=o[:, jj, :], in0=S[("p2", pr, jj)][:], in1=bf_b[:], op=ALU.add)
+
+        def st_h2(pr):
+            o = S[("o", pr)]
+            if RELU_ENGINE == "G":
+                nc.gpsimd.tensor_scalar(out=o[:], in0=o[:], scalar1=BIG, scalar2=0.0, op0=ALU.min, op1=ALU.max)
+            for jj in range(2):
+                if RELU_ENGINE == "G":
+                    continue
+                if RELU_ENGINE == "S":
+                    nc.scalar.activation(out=o[:, jj, :], in_=o[:, jj, :], func=ACT.Relu)
+                else:
+                    nc.vector.tensor_scalar(out=o[:, jj, :], in0=o[:, jj, :], scalar1=0.0, scalar2=None, op0=ALU.max)
+            j0 = (pr % 4) * 2
+            nc.sync.dma_start(out=ov[pr // 4][:, j0:j0 + 2, :], in_=o[:])
+
+        def on(fn, pr):
+            if 0 <= pr < NPAIR:
+                fn(pr)
+
+        for n in range(NPAIR + 8):
+            if n % 4 == 1 and n // 4 + 3 < NCH:
+                load_h(n // 4 + 3, 1)
+                load_x(n // 4 + 3, 1)
+            on(st_xp, n)
+            on(st_c, n - 3)
+            on(st_mx1, n - 2)
+            on(st_h1, n - 7)
+            on(st_mx2, n - 6)
+            on(st_a, n - 1)
+            on(st_f, n - 5)
+            on(st_e, n - 4)
+            on(st_th, n)
+            on(st_tz, n - 4)
+            on(st_d, n - 3)
+            on(st_f2, n - 5)
+            on(st_qh, n - 1)
+            on(st_qx, n - 5)
+            on(st_h2, n - 7)

@@ -21,9 +21,9 @@ EPS = 1e-5
 FLOPS = 2 * 2 * TOKENS * DIM * DIM
 
 MANUAL = True
-XP_ENGINE = "G"
+XP_ENGINE = "V"
 E_ENGINE = "V"
-RELU_ENGINE = "G"
+RELU_ENGINE = "S"
 BIG = 3.0e38
 
 
@@ -233,13 +233,10 @@ def tile_l1regressionmoeactionhead_pc_t_kernel(tc, h_attn, x, W_o, b_o, W_ffn, b
             o = S[("o", pr)]
             if RELU_ENGINE == "G":
                 nc.gpsimd.tensor_scalar(out=o[:], in0=o[:], scalar1=BIG, scalar2=0.0, op0=ALU.min, op1=ALU.max)
-            for jj in range(2):
-                if RELU_ENGINE == "G":
-                    continue
-                if RELU_ENGINE == "S":
-                    nc.scalar.activation(out=o[:, jj, :], in_=o[:, jj, :], func=ACT.Relu)
-                else:
-                    nc.vector.tensor_scalar(out=o[:, jj, :], in0=o[:, jj, :], scalar1=0.0, scalar2=None, op0=ALU.max)
+            elif RELU_ENGINE == "S":
+                nc.scalar.activation(out=o[:], in_=o[:], func=ACT.Relu)
+            else:
+                nc.vector.tensor_scalar(out=o[:], in0=o[:], scalar1=0.0, scalar2=None, op0=ALU.max)
             j0 = (pr % 4) * 2
             nc.sync.dma_start(out=ov[pr // 4][:, j0:j0 + 2, :], in_=o[:])
 

@@ -21,7 +21,7 @@ EPS = 1e-5
 FLOPS = 2 * 2 * TOKENS * DIM * DIM
 
 MANUAL = True
-XP_ENGINE = "V"
+XP_ENGINE = "G"
 E_ENGINE = "V"
 RELU_ENGINE = "S"
 BIG = 3.0e38
@@ -120,7 +120,7 @@ def tile_l1regressionmoeactionhead_pc_t_kernel(tc, h_attn, x, W_o, b_o, W_ffn, b
             return tiles[pr // 4][:, (pr % 4) * 2 + jj, :]
 
         def st_xp(pr):
-            xp = work.tile([P, 2, DIM], F32, tag="xp", bufs=4, name="xp")
+            xp = work.tile([P, 2, DIM], F32, tag="xp", bufs=6, name="xp")
             j0 = (pr % 4) * 2
             eng = nc.gpsimd if XP_ENGINE == "G" else nc.vector
             eng.tensor_tensor(out=xp[:], in0=x_tiles[pr // 4][:, j0:j0 + 2, :], in1=bo_b[:].unsqueeze(1).to_broadcast([P, 2, DIM]), op=ALU.add)
@@ -135,7 +135,7 @@ def tile_l1regressionmoeactionhead_pc_t_kernel(tc, h_attn, x, W_o, b_o, W_ffn, b
                     nc.tensor.transpose(ht[:, jj, u, :], src(h_tiles, pr, jj).bitcast(F32)[:, u * P:(u + 1) * P], ident_f[:])
 
         def st_a(pr):
-            hg = work.tile([P, 2 * DIM], BF16, tag="hg", align_bytes=64, name="hg")
+            hg = work.tile([P, 2 * DIM], BF16, tag="hg", bufs=3, align_bytes=64, name="hg")
             S[("hg", pr)] = hg
             nc.scalar.copy(out=hg[:].bitcast(F32).rearrange("p (j r u) -> p j r u", j=2, u=2),
                            in_=S[("ht", pr)][:].rearrange("p j u r -> p j r u"))
@@ -156,29 +156,39 @@ def tile_l1regressionmoeactionhead_pc_t_kernel(tc, h_attn, x, W_o, b_o, W_ffn, b
 
         def st_c(pr):
             sums = stats.tile([P, 2], F32, tag="sums", name="sums")
+            S[("sums", pr)] = sums
             for jj in range(2):
                 y = work.tile([P, DIM], F32, tag="y", bufs=8, name="y")
                 S[("y", pr, jj)] = y
                 nc.vector.scalar_tensor_tensor(out=y[:], in0=S[("p1", pr, jj)][:], scalar=0.0, in1=S[("xp", pr, jj)],
                                                op0=ALU.add, op1=ALU.add, accum_out=sums[:, jj:jj + 1])
+
+        def st_negmu(pr):
             negmu = stats.tile([P, 2], F32, tag="negmu", name="negmu")
             S[("negmu", pr)] = negmu
-            nc.vector.tensor_scalar(out=negmu[:], in0=sums[:], scalar1=-1.0 / DIM, scalar2=None, op0=ALU.mult)
+            nc.vector.tensor_scalar(out=negmu[:], in0=S[("sums", pr)][:], scalar1=-1.0 / DIM, scalar2=None, op0=ALU.mult)
 
         def st_d(pr):
             ssq = stats.tile([P, 2], F32, tag="ssq", name="ssq")
+            S[("ssq", pr)] = ssq
             negmu = S[("negmu", pr)]
             for jj in range(2):
                 junk = work.tile([P, DIM], BF16, tag="junk", name="junk")
                 nc.scalar.activation(out=junk[:], in_=S[("y", pr, jj)][:], func=ACT.Square, bias=negmu[:, jj:jj + 1], scale=1.0,
                                      accum_out=ssq[:, jj:jj + 1])
+
+        def st_sqrt(pr):
             std = stats.tile([P, 2], F32, tag="std", name="std")
             S[("std", pr)] = std
-            nc.scalar.activation(out=std[:], in_=ssq[:], func=ACT.Sqrt, bias=eps_t[:, 0:1], scale=1.0 / DIM)
+            nc.scalar.activation(out=std[:], in_=S[("ssq", pr)][:], func=ACT.Sqrt, bias=eps_t[:, 0:1], scale=1.0 / DIM)
+
+        def st_recip(pr):
+            rstd = stats.tile([P, 2], F32, tag="rstd", name="rstd")
+            S[("rstd", pr)] = rstd
+            nc.vector.reciprocal(out=rstd[:], in_=S[("std", pr)][:])
 
         def st_e(pr):
-            rstd = stats.tile([P, 2], F32, tag="rstd", name="rstd")
-            nc.vector.reciprocal(out=rstd[:], in_=S[("std", pr)][:])
+            rstd = S[("rstd", pr)]
             negmu = S[("negmu", pr)]
             for jj in range(2):
                 y = S[("y", pr, jj)]
@@ -195,7 +205,7 @@ def tile_l1regressionmoeactionhead_pc_t_kernel(tc, h_attn, x, W_o, b_o, W_ffn, b
                         nc.tensor.transpose(zt[:, tt, jj, :], S[("y", pr, jj)][:, t * P:(t + 1) * P], ident_f[:])
 
         def st_f(pr):
-            planes = work.tile([P, 4, 2 * P], BF16, tag="planes", name="planes")
+            planes = work.tile([P, 4, 2 * P], BF16, tag="planes", bufs=3, name="planes")
             S[("planes", pr)] = planes
             for b in range(2):
                 for tt in range(2):
@@ -204,7 +214,7 @@ def tile_l1regressionmoeactionhead_pc_t_kernel(tc, h_attn, x, W_o, b_o, W_ffn, b
                                          func=ACT.Identity, bias=gb[:, 4 + t:5 + t], scale=gb[:, t:t + 1])
 
         def st_f2(pr):
-            xg = work.tile([P, 2 * P, 4], BF16, tag="xg", align_bytes=64, name="xg")
+            xg = work.tile([P, 2 * P, 4], BF16, tag="xg", bufs=3, align_bytes=64, name="xg")
             S[("xg", pr)] = xg
             nc.vector.tensor_copy(out=xg[:].rearrange("p (c i) t -> p c t i", i=4),
                                   in_=S[("planes", pr)][:].rearrange("p t (c i) -> p c t i", i=4))
@@ -244,22 +254,25 @@ def tile_l1regressionmoeactionhead_pc_t_kernel(tc, h_attn, x, W_o, b_o, W_ffn, b
             if 0 <= pr < NPAIR:
                 fn(pr)
 
-        for n in range(NPAIR + 8):
+        for n in range(NPAIR + 13):
             if n % 4 == 1 and n // 4 + 3 < NCH:
                 load_h(n // 4 + 3, 1)
                 load_x(n // 4 + 3, 1)
+            on(st_recip, n - 6)
+            on(st_qx, n - 9)
             on(st_xp, n)
-            on(st_c, n - 3)
-            on(st_mx1, n - 2)
-            on(st_h1, n - 7)
-            on(st_mx2, n - 6)
+            on(st_c, n - 4)
+            on(st_mx1, n - 3)
+            on(st_qh, n - 2)
+            on(st_negmu, n - 4)
+            on(st_h1, n - 11)
+            on(st_mx2, n - 10)
             on(st_a, n - 1)
-            on(st_f, n - 5)
-            on(st_e, n - 4)
+            on(st_f, n - 7)
+            on(st_e, n - 6)
             on(st_th, n)
-            on(st_tz, n - 4)
-            on(st_d, n - 3)
-            on(st_f2, n - 5)
-            on(st_qh, n - 1)
-            on(st_qx, n - 5)
-            on(st_h2, n - 7)
+            on(st_tz, n - 6)
+            on(st_d, n - 5)
+            on(st_f2, n - 8)
+            on(st_h2, n - 12)
+            on(st_sqrt, n - 5)

@@ -21,10 +21,7 @@ EPS = 1e-5
 FLOPS = 2 * 2 * TOKENS * DIM * DIM
 
 MANUAL = True
-XP_ENGINE = "G"
-E_ENGINE = "V"
-RELU_ENGINE = "S"
-BIG = 3.0e38
+NQUAD = NPAIR // 2
 
 
 def tile_l1regressionmoeactionhead_pc_t_kernel(tc, h_attn, x, W_o, b_o, W_ffn, b_ffn, gamma, beta, out):
@@ -35,7 +32,7 @@ def tile_l1regressionmoeactionhead_pc_t_kernel(tc, h_attn, x, W_o, b_o, W_ffn, b
 
     with ExitStack() as ctx:
         const = ctx.enter_context(tc.tile_pool(name="const", bufs=1))
-        loads = ctx.enter_context(tc.tile_pool(name="loads", bufs=4))
+        loads = ctx.enter_context(tc.tile_pool(name="loads", bufs=3))
         work = ctx.enter_context(tc.tile_pool(name="work", bufs=2))
         stats = ctx.enter_context(tc.tile_pool(name="stats", bufs=4))
         psum = ctx.enter_context(tc.psum_pool(name="psum", bufs=2))
@@ -116,84 +113,97 @@ def tile_l1regressionmoeactionhead_pc_t_kernel(tc, h_attn, x, W_o, b_o, W_ffn, b
 
         S = {}
 
-        def src(tiles, pr, jj):
-            return tiles[pr // 4][:, (pr % 4) * 2 + jj, :]
-
-        def st_xp(pr):
-            xp = work.tile([P, 2, DIM], F32, tag="xp", bufs=6, name="xp")
-            j0 = (pr % 4) * 2
-            eng = nc.gpsimd if XP_ENGINE == "G" else nc.vector
-            eng.tensor_tensor(out=xp[:], in0=x_tiles[pr // 4][:, j0:j0 + 2, :], in1=bo_b[:].unsqueeze(1).to_broadcast([P, 2, DIM]), op=ALU.add)
-            for jj in range(2):
-                S[("xp", pr, jj)] = xp[:, jj, :]
+        def st_xp(q):
+            xp = work.tile([P, 4, DIM], F32, tag="xp", bufs=3, name="xp")
+            S[("xp", q)] = xp
+            j0 = (q % 2) * 4
+            nc.vector.tensor_tensor(out=xp[:], in0=x_tiles[q // 2][:, j0:j0 + 4, :], in1=bo_b[:].unsqueeze(1).to_broadcast([P, 4, DIM]), op=ALU.add)
 
         def st_th(pr):
             ht = psum.tile([P, 2, 2, P], F32, tag="ht", name="ht")
             S[("ht", pr)] = ht
             for jj in range(2):
+                hsrc = h_tiles[pr // 4][:, (pr % 4) * 2 + jj, :]
                 for u in range(2):
-                    nc.tensor.transpose(ht[:, jj, u, :], src(h_tiles, pr, jj).bitcast(F32)[:, u * P:(u + 1) * P], ident_f[:])
+                    nc.tensor.transpose(ht[:, jj, u, :], hsrc.bitcast(F32)[:, u * P:(u + 1) * P], ident_f[:])
 
         def st_a(pr):
-            hg = work.tile([P, 2 * DIM], BF16, tag="hg", bufs=3, align_bytes=64, name="hg")
-            S[("hg", pr)] = hg
-            nc.scalar.copy(out=hg[:].bitcast(F32).rearrange("p (j r u) -> p j r u", j=2, u=2),
+            q = pr // 2
+            if pr % 2 == 0:
+                hg_new = work.tile([P, 4 * DIM], BF16, tag="hg", bufs=3, align_bytes=64, name="hg")
+                S[("hg", q)] = hg_new
+            hg = S[("hg", q)]
+            j0 = (pr % 2) * 2
+            nc.scalar.copy(out=hg[:].bitcast(F32).rearrange("p (j r u) -> p j r u", j=4, u=2)[:, j0:j0 + 2, :, :],
                            in_=S[("ht", pr)][:].rearrange("p j u r -> p j r u"))
 
-        def st_qh(pr):
-            hc = work.tile([P, 2 * P], U32, tag="hc", bufs=3, align_bytes=64, name="hc")
-            hs = work.tile([P, 2 * P], U8, tag="hs", bufs=3, align_bytes=64, name="hs")
-            S[("hc", pr)] = (hc, hs)
-            nc.vector.quantize_mx(out=hc[:].bitcast(FP8X4), scales=hs[:], in_=S[("hg", pr)][:])
+        def st_qh(q):
+            hc = work.tile([P, 4 * P], U32, tag="hc", bufs=3, align_bytes=64, name="hc")
+            hs = work.tile([P, 4 * P], U8, tag="hs", bufs=3, align_bytes=64, name="hs")
+            S[("hc", q)] = (hc, hs)
+            nc.vector.quantize_mx(out=hc[:].bitcast(FP8X4), scales=hs[:], in_=S[("hg", q)][:])
 
         def st_mx1(pr):
-            hc, hs = S[("hc", pr)]
+            hc, hs = S[("hc", pr // 2)]
             for jj in range(2):
+                c0 = ((pr % 2) * 2 + jj) * P
                 p1 = psum.tile([P, DIM], F32, tag="p1", name="p1")
                 S[("p1", pr, jj)] = p1
-                nc.tensor.matmul_mx(out=p1[:], lhsT=hc[:, jj * P:(jj + 1) * P].bitcast(FP8X4), lhsT_scale=hs[:, jj * P:(jj + 1) * P],
+                nc.tensor.matmul_mx(out=p1[:], lhsT=hc[:, c0:c0 + P].bitcast(FP8X4), lhsT_scale=hs[:, c0:c0 + P],
                                     rhs=woc[:].bitcast(FP8X4), rhs_scale=wos[:], start=True, stop=True)
 
         def st_c(pr):
-            sums = stats.tile([P, 2], F32, tag="sums", name="sums")
-            S[("sums", pr)] = sums
+            q = pr // 2
+            if pr % 2 == 0:
+                sums_new = stats.tile([P, 4], F32, tag="sums", name="sums")
+                S[("sums", q)] = sums_new
+            sums = S[("sums", q)]
             for jj in range(2):
-                y = work.tile([P, DIM], F32, tag="y", bufs=8, name="y")
+                j = (pr % 2) * 2 + jj
+                y = work.tile([P, DIM], F32, tag="y", bufs=14, name="y")
                 S[("y", pr, jj)] = y
-                nc.vector.scalar_tensor_tensor(out=y[:], in0=S[("p1", pr, jj)][:], scalar=0.0, in1=S[("xp", pr, jj)],
-                                               op0=ALU.add, op1=ALU.add, accum_out=sums[:, jj:jj + 1])
+                nc.vector.scalar_tensor_tensor(out=y[:], in0=S[("p1", pr, jj)][:], scalar=0.0, in1=S[("xp", q)][:, j, :],
+                                               op0=ALU.add, op1=ALU.add, accum_out=sums[:, j:j + 1])
 
-        def st_negmu(pr):
-            negmu = stats.tile([P, 2], F32, tag="negmu", name="negmu")
-            S[("negmu", pr)] = negmu
-            nc.vector.tensor_scalar(out=negmu[:], in0=S[("sums", pr)][:], scalar1=-1.0 / DIM, scalar2=None, op0=ALU.mult)
+        def st_negmu(q):
+            negmu = stats.tile([P, 4], F32, tag="negmu", name="negmu")
+            S[("negmu", q)] = negmu
+            nc.vector.tensor_scalar(out=negmu[:], in0=S[("sums", q)][:], scalar1=-1.0 / DIM, scalar2=None, op0=ALU.mult)
 
         def st_d(pr):
-            ssq = stats.tile([P, 2], F32, tag="ssq", name="ssq")
-            S[("ssq", pr)] = ssq
-            negmu = S[("negmu", pr)]
+            q = pr // 2
+            if pr % 2 == 0:
+                ssq_new = stats.tile([P, 4], F32, tag="ssq", name="ssq")
+                S[("ssq", q)] = ssq_new
+            ssq = S[("ssq", q)]
+            negmu = S[("negmu", q)]
             for jj in range(2):
+                j = (pr % 2) * 2 + jj
                 junk = work.tile([P, DIM], BF16, tag="junk", name="junk")
-                nc.scalar.activation(out=junk[:], in_=S[("y", pr, jj)][:], func=ACT.Square, bias=negmu[:, jj:jj + 1], scale=1.0,
-                                     accum_out=ssq[:, jj:jj + 1])
+                nc.scalar.activation(out=junk[:], in_=S[("y", pr, jj)][:], func=ACT.Square, bias=negmu[:, j:j + 1], scale=1.0,
+                                     accum_out=ssq[:, j:j + 1])
 
-        def st_sqrt(pr):
-            std = stats.tile([P, 2], F32, tag="std", name="std")
-            S[("std", pr)] = std
-            nc.scalar.activation(out=std[:], in_=S[("ssq", pr)][:], func=ACT.Sqrt, bias=eps_t[:, 0:1], scale=1.0 / DIM)
+        def st_sqrt(q):
+            std = stats.tile([P, 4], F32, tag="std", name="std")
+            S[("std", q)] = std
+            nc.scalar.activation(out=std[:], in_=S[("ssq", q)][:], func=ACT.Sqrt, bias=eps_t[:, 0:1], scale=1.0 / DIM)
 
-        def st_recip(pr):
-            rstd = stats.tile([P, 2], F32, tag="rstd", name="rstd")
-            S[("rstd", pr)] = rstd
-            nc.vector.reciprocal(out=rstd[:], in_=S[("std", pr)][:])
+        def st_recip(q):
+            rstd = stats.tile([P, 4], F32, tag="rstd", name="rstd")
+            S[("rstd", q)] = rstd
+            nc.vector.reciprocal(out=rstd[:], in_=S[("std", q)][:])
+
+        def st_nmr(q):
+            nmr = stats.tile([P, 4], F32, tag="nmr", name="nmr")
+            S[("nmr", q)] = nmr
+            nc.vector.tensor_tensor(out=nmr[:], in0=S[("negmu", q)][:], in1=S[("rstd", q)][:], op=ALU.mult)
 
         def st_e(pr):
-            rstd = S[("rstd", pr)]
-            negmu = S[("negmu", pr)]
+            q = pr // 2
             for jj in range(2):
+                j = (pr % 2) * 2 + jj
                 y = S[("y", pr, jj)]
-                eng = nc.vector if E_ENGINE == "V" else nc.gpsimd
-                eng.tensor_scalar(out=y[:], in0=y[:], scalar1=negmu[:, jj:jj + 1], scalar2=rstd[:, jj:jj + 1], op0=ALU.add, op1=ALU.mult)
+                nc.scalar.activation(out=y[:], in_=y[:], func=ACT.Identity, bias=S[("nmr", q)][:, j:j + 1], scale=S[("rstd", q)][:, j:j + 1])
 
         def st_tz(pr):
             for b in range(2):
@@ -205,74 +215,85 @@ def tile_l1regressionmoeactionhead_pc_t_kernel(tc, h_attn, x, W_o, b_o, W_ffn, b
                         nc.tensor.transpose(zt[:, tt, jj, :], S[("y", pr, jj)][:, t * P:(t + 1) * P], ident_f[:])
 
         def st_f(pr):
-            planes = work.tile([P, 4, 2 * P], BF16, tag="planes", bufs=3, name="planes")
-            S[("planes", pr)] = planes
+            q = pr // 2
+            if pr % 2 == 0:
+                planes_new = work.tile([P, 4, 4 * P], BF16, tag="planes", bufs=3, name="planes")
+                S[("planes", q)] = planes_new
+            planes = S[("planes", q)]
+            c0 = (pr % 2) * 2 * P
             for b in range(2):
                 for tt in range(2):
                     t = 2 * b + tt
-                    nc.scalar.activation(out=planes[:, t, :], in_=S[("zt", pr, b)][:, tt, :, :].rearrange("p j r -> p (j r)"),
+                    nc.scalar.activation(out=planes[:, t, c0:c0 + 2 * P], in_=S[("zt", pr, b)][:, tt, :, :].rearrange("p j r -> p (j r)"),
                                          func=ACT.Identity, bias=gb[:, 4 + t:5 + t], scale=gb[:, t:t + 1])
 
-        def st_f2(pr):
-            xg = work.tile([P, 2 * P, 4], BF16, tag="xg", bufs=3, align_bytes=64, name="xg")
-            S[("xg", pr)] = xg
+        def st_f2(q):
+            xg = work.tile([P, 4 * P, 4], BF16, tag="xg", bufs=2, align_bytes=64, name="xg")
+            S[("xg", q)] = xg
             nc.vector.tensor_copy(out=xg[:].rearrange("p (c i) t -> p c t i", i=4),
-                                  in_=S[("planes", pr)][:].rearrange("p t (c i) -> p c t i", i=4))
+                                  in_=S[("planes", q)][:].rearrange("p t (c i) -> p c t i", i=4))
 
-        def st_qx(pr):
-            xc = work.tile([P, 2 * P], U32, tag="xc", bufs=3, align_bytes=64, name="xc")
-            xs = work.tile([P, 2 * P], U8, tag="xs", bufs=3, align_bytes=64, name="xs")
-            S[("xc", pr)] = (xc, xs)
-            nc.vector.quantize_mx(out=xc[:].bitcast(FP8X4), scales=xs[:], in_=S[("xg", pr)][:].rearrange("p c t -> p (c t)"))
+        def st_qx(q):
+            xc = work.tile([P, 4 * P], U32, tag="xc", bufs=3, align_bytes=64, name="xc")
+            xs = work.tile([P, 4 * P], U8, tag="xs", bufs=3, align_bytes=64, name="xs")
+            S[("xc", q)] = (xc, xs)
+            nc.vector.quantize_mx(out=xc[:].bitcast(FP8X4), scales=xs[:], in_=S[("xg", q)][:].rearrange("p c t -> p (c t)"))
 
         def st_mx2(pr):
-            xc, xs = S[("xc", pr)]
+            xc, xs = S[("xc", pr // 2)]
             for jj in range(2):
+                c0 = ((pr % 2) * 2 + jj) * P
                 p2 = psum.tile([P, DIM], F32, tag="p2", name="p2")
                 S[("p2", pr, jj)] = p2
-                nc.tensor.matmul_mx(out=p2[:], lhsT=xc[:, jj * P:(jj + 1) * P].bitcast(FP8X4), lhsT_scale=xs[:, jj * P:(jj + 1) * P],
+                nc.tensor.matmul_mx(out=p2[:], lhsT=xc[:, c0:c0 + P].bitcast(FP8X4), lhsT_scale=xs[:, c0:c0 + P],
                                     rhs=wfc[:].bitcast(FP8X4), rhs_scale=wfs[:], start=True, stop=True)
 
         def st_h1(pr):
-            o = work.tile([P, 2, DIM], F32, tag="o", bufs=4, name="o")
-            S[("o", pr)] = o
+            q = pr // 2
+            if pr % 2 == 0:
+                o_new = work.tile([P, 4, DIM], F32, tag="o", bufs=3, name="o")
+                S[("o", q)] = o_new
+            o = S[("o", q)]
             for jj in range(2):
-                nc.vector.tensor_tensor(out=o[:, jj, :], in0=S[("p2", pr, jj)][:], in1=bf_b[:], op=ALU.add)
+                nc.vector.tensor_tensor(out=o[:, (pr % 2) * 2 + jj, :], in0=S[("p2", pr, jj)][:], in1=bf_b[:], op=ALU.add)
 
-        def st_h2(pr):
-            o = S[("o", pr)]
-            if RELU_ENGINE == "G":
-                nc.gpsimd.tensor_scalar(out=o[:], in0=o[:], scalar1=BIG, scalar2=0.0, op0=ALU.min, op1=ALU.max)
-            elif RELU_ENGINE == "S":
-                nc.scalar.activation(out=o[:], in_=o[:], func=ACT.Relu)
-            else:
+        def st_relu(q):
+            o = S[("o", q)]
+            if q % 2 == 0:
                 nc.vector.tensor_scalar(out=o[:], in0=o[:], scalar1=0.0, scalar2=None, op0=ALU.max)
-            j0 = (pr % 4) * 2
-            nc.sync.dma_start(out=ov[pr // 4][:, j0:j0 + 2, :], in_=o[:])
+            else:
+                nc.scalar.activation(out=o[:], in_=o[:], func=ACT.Relu)
+            j0 = (q % 2) * 4
+            nc.sync.dma_start(out=ov[q // 2][:, j0:j0 + 4, :], in_=o[:])
 
         def on(fn, pr):
             if 0 <= pr < NPAIR:
                 fn(pr)
 
-        for n in range(NPAIR + 13):
-            if n % 4 == 1 and n // 4 + 3 < NCH:
-                load_h(n // 4 + 3, 1)
-                load_x(n // 4 + 3, 1)
-            on(st_recip, n - 6)
-            on(st_qx, n - 9)
-            on(st_xp, n)
-            on(st_c, n - 4)
-            on(st_mx1, n - 3)
-            on(st_qh, n - 2)
-            on(st_negmu, n - 4)
-            on(st_h1, n - 11)
-            on(st_mx2, n - 10)
+        def onq(fn, m):
+            if m % 2 == 0 and 0 <= m // 2 < NQUAD:
+                fn(m // 2)
+
+        for n in range(NPAIR + 20):
+            if n % 4 == 1 and n >= 5 and n // 4 + 2 < NCH:
+                load_h(n // 4 + 2, 1)
+                load_x(n // 4 + 2, 1)
+            onq(st_recip, n - 9)
+            onq(st_xp, n - 2)
+            onq(st_qx, n - 14)
+            on(st_c, n - 5)
+            on(st_mx1, n - 4)
+            onq(st_qh, n - 3)
+            on(st_h1, n - 16)
+            on(st_mx2, n - 15)
+            onq(st_negmu, n - 6)
+            onq(st_nmr, n - 9)
+            on(st_e, n - 10)
             on(st_a, n - 1)
-            on(st_f, n - 7)
-            on(st_e, n - 6)
             on(st_th, n)
-            on(st_tz, n - 6)
-            on(st_d, n - 5)
-            on(st_f2, n - 8)
-            on(st_h2, n - 12)
-            on(st_sqrt, n - 5)
+            on(st_d, n - 7)
+            on(st_f, n - 11)
+            on(st_tz, n - 10)
+            onq(st_sqrt, n - 8)
+            onq(st_f2, n - 13)
+            onq(st_relu, n - 19)

@@ -56,22 +56,22 @@ def tile_l1regressionmoeactionhead_pc_t_kernel(tc, h_attn, x, W_o, b_o, W_ffn, b
             for i in range(pieces):
                 nc.sync.dma_start(out=x_sb[:, i * step:(i + 1) * step, :], in_=xv[c][:, i * step:(i + 1) * step, :])
 
+        bo_b = const.tile([P, DIM], BF16)
+        nc.scalar.dma_start(out=bo_b[:], in_=b_o.partition_broadcast(P))
+        load_x(0, 2)
         wo_sb = const.tile([P, 4, DIM], BF16)
         nc.sync.dma_start(out=wo_sb[:], in_=W_o.rearrange("(r p) k -> p r k", p=P))
         load_h(0, 4)
-        bo_b = const.tile([P, DIM], BF16)
-        nc.scalar.dma_start(out=bo_b[:], in_=b_o.partition_broadcast(P))
         gbr = const.tile([P, P], BF16)
         nc.vector.memset(gbr[:], 0.0)
         nc.scalar.dma_start(out=gbr[0:4, :], in_=gamma.rearrange("(t p) -> t p", p=P))
         nc.scalar.dma_start(out=gbr[4:8, :], in_=beta.rearrange("(t p) -> t p", p=P))
-        load_x(0, 4)
         wf_sb = const.tile([P, 4, DIM], BF16)
         nc.sync.dma_start(out=wf_sb[:], in_=W_ffn.rearrange("(r p) k -> p r k", p=P))
+        load_x(1, 2)
         bf_b = const.tile([P, DIM], BF16)
         nc.scalar.dma_start(out=bf_b[:], in_=b_ffn.partition_broadcast(P))
         load_h(1, 1)
-        load_x(1, 1)
         load_h(2, 1)
         load_x(2, 1)
 
@@ -82,7 +82,17 @@ def tile_l1regressionmoeactionhead_pc_t_kernel(tc, h_attn, x, W_o, b_o, W_ffn, b
         eps_t = const.tile([P, 1], F32)
         nc.vector.memset(eps_t[:], EPS)
         warm = const.tile([P, 1], F32)
-        nc.scalar.activation(out=warm[:], in_=eps_t[:], func=ACT.Sqrt)
+        nc.scalar.activation(out=warm[:], in_=eps_t[:], func=ACT.Abs_reciprocal_sqrt)
+
+        S = {}
+
+        def st_xp(q):
+            xp = work.tile([P, 4, DIM], F32, tag="xp", bufs=3, name="xp")
+            S[("xp", q)] = xp
+            j0 = (q % 2) * 4
+            nc.vector.tensor_tensor(out=xp[:], in0=x_tiles[q // 2][:, j0:j0 + 4, :], in1=bo_b[:].unsqueeze(1).to_broadcast([P, 4, DIM]), op=ALU.add)
+
+        st_xp(0)
 
         wog = const.tile([P, DIM * 4], BF16, align_bytes=64)
         woc = const.tile([P, DIM], U32, align_bytes=64)
@@ -93,31 +103,28 @@ def tile_l1regressionmoeactionhead_pc_t_kernel(tc, h_attn, x, W_o, b_o, W_ffn, b
             for rr in range(2):
                 for u in range(2):
                     nc.tensor.transpose(wt[:, rr, u, :], wo_sb[:, 2 * half + rr, :].bitcast(F32)[:, u * P:(u + 1) * P], ident_f[:])
-            nc.vector.tensor_copy(out=wog_w[:, 2 * half:2 * half + 2, :, :], in_=wt[:].rearrange("p j u r -> p j r u"))
+            nc.scalar.copy(out=wog_w[:, 2 * half:2 * half + 2, :, :], in_=wt[:].rearrange("p j u r -> p j r u"))
         nc.vector.quantize_mx(out=woc[:].bitcast(FP8X4), scales=wos[:], in_=wog[:])
+        st_xp(1)
 
-        gb_ps = psum.tile([P, P], BF16, tag="zt", name="gb_ps")
-        nc.tensor.transpose(gb_ps[:], gbr[:], ident_b[:])
         gb = const.tile([P, 8], F32)
-        nc.vector.tensor_copy(out=gb[:], in_=gb_ps[:, 0:8])
-
         wfg = const.tile([P, DIM, 4], BF16, align_bytes=64)
         wfc = const.tile([P, DIM], U32, align_bytes=64)
         wfs = const.tile([P, DIM], U8, align_bytes=64)
-        for r in range(4):
-            wt2 = psum.tile([P, 4, P], BF16, tag="p2", name="wt2")
-            for t in range(4):
-                nc.tensor.transpose(wt2[:, t, :], wf_sb[:, r, t * P:(t + 1) * P], ident_b[:])
-            nc.scalar.copy(out=wfg[:, r * P:(r + 1) * P, :], in_=wt2[:].rearrange("p t c -> p c t"))
-        nc.vector.quantize_mx(out=wfc[:].bitcast(FP8X4), scales=wfs[:], in_=wfg[:].rearrange("p c t -> p (c t)"))
 
-        S = {}
+        def prep_wf_transposes():
+            gb_ps = psum.tile([P, P], BF16, tag="zt", name="gb_ps")
+            S["gb_ps"] = gb_ps
+            nc.tensor.transpose(gb_ps[:], gbr[:], ident_b[:])
+            for r in range(4):
+                wt2 = psum.tile([P, 4, P], BF16, tag="p2", name="wt2")
+                for t in range(4):
+                    nc.tensor.transpose(wt2[:, t, :], wf_sb[:, r, t * P:(t + 1) * P], ident_b[:])
+                nc.scalar.copy(out=wfg[:, r * P:(r + 1) * P, :], in_=wt2[:].rearrange("p t c -> p c t"))
 
-        def st_xp(q):
-            xp = work.tile([P, 4, DIM], F32, tag="xp", bufs=3, name="xp")
-            S[("xp", q)] = xp
-            j0 = (q % 2) * 4
-            nc.vector.tensor_tensor(out=xp[:], in0=x_tiles[q // 2][:, j0:j0 + 4, :], in1=bo_b[:].unsqueeze(1).to_broadcast([P, 4, DIM]), op=ALU.add)
+        def prep_wf_quantise():
+            nc.vector.tensor_copy(out=gb[:], in_=S["gb_ps"][:, 0:8])
+            nc.vector.quantize_mx(out=wfc[:].bitcast(FP8X4), scales=wfs[:], in_=wfg[:].rearrange("p c t -> p (c t)"))
 
         def st_th(pr):
             ht = psum.tile([P, 2, 2, P], F32, tag="ht", name="ht")
@@ -130,7 +137,7 @@ def tile_l1regressionmoeactionhead_pc_t_kernel(tc, h_attn, x, W_o, b_o, W_ffn, b
         def st_a(pr):
             q = pr // 2
             if pr % 2 == 0:
-                hg_new = work.tile([P, 4 * DIM], BF16, tag="hg", bufs=3, align_bytes=64, name="hg")
+                hg_new = work.tile([P, 4 * DIM], BF16, tag="hg", bufs=4, align_bytes=64, name="hg")
                 S[("hg", q)] = hg_new
             hg = S[("hg", q)]
             j0 = (pr % 2) * 2
@@ -168,7 +175,7 @@ def tile_l1regressionmoeactionhead_pc_t_kernel(tc, h_attn, x, W_o, b_o, W_ffn, b
         def st_negmu(q):
             negmu = stats.tile([P, 4], F32, tag="negmu", name="negmu")
             S[("negmu", q)] = negmu
-            nc.vector.tensor_scalar(out=negmu[:], in0=S[("sums", q)][:], scalar1=-1.0 / DIM, scalar2=None, op0=ALU.mult)
+            nc.gpsimd.tensor_scalar(out=negmu[:], in0=S[("sums", q)][:], scalar1=-1.0 / DIM, scalar2=0.0, op0=ALU.mult, op1=ALU.add)
 
         def st_d(pr):
             q = pr // 2
@@ -183,20 +190,15 @@ def tile_l1regressionmoeactionhead_pc_t_kernel(tc, h_attn, x, W_o, b_o, W_ffn, b
                 nc.scalar.activation(out=junk[:], in_=S[("y", pr, jj)][:], func=ACT.Square, bias=negmu[:, j:j + 1], scale=1.0,
                                      accum_out=ssq[:, j:j + 1])
 
-        def st_sqrt(q):
-            std = stats.tile([P, 4], F32, tag="std", name="std")
-            S[("std", q)] = std
-            nc.scalar.activation(out=std[:], in_=S[("ssq", q)][:], func=ACT.Sqrt, bias=eps_t[:, 0:1], scale=1.0 / DIM)
-
-        def st_recip(q):
+        def st_ars(q):
             rstd = stats.tile([P, 4], F32, tag="rstd", name="rstd")
             S[("rstd", q)] = rstd
-            nc.vector.reciprocal(out=rstd[:], in_=S[("std", q)][:])
+            nc.scalar.activation(out=rstd[:], in_=S[("ssq", q)][:], func=ACT.Abs_reciprocal_sqrt, bias=eps_t[:, 0:1], scale=1.0 / DIM)
 
         def st_nmr(q):
             nmr = stats.tile([P, 4], F32, tag="nmr", name="nmr")
             S[("nmr", q)] = nmr
-            nc.vector.tensor_tensor(out=nmr[:], in0=S[("negmu", q)][:], in1=S[("rstd", q)][:], op=ALU.mult)
+            nc.gpsimd.tensor_tensor(out=nmr[:], in0=S[("negmu", q)][:], in1=S[("rstd", q)][:], op=ALU.mult)
 
         def st_e(pr):
             q = pr // 2
@@ -259,12 +261,22 @@ def tile_l1regressionmoeactionhead_pc_t_kernel(tc, h_attn, x, W_o, b_o, W_ffn, b
 
         def st_relu(q):
             o = S[("o", q)]
-            if q % 2 == 0:
+            j0 = (q % 2) * 4
+            if q == NQUAD - 1:
+                return
+            if q % 4 == 1:
                 nc.vector.tensor_scalar(out=o[:], in0=o[:], scalar1=0.0, scalar2=None, op0=ALU.max)
             else:
                 nc.scalar.activation(out=o[:], in_=o[:], func=ACT.Relu)
-            j0 = (q % 2) * 4
             nc.sync.dma_start(out=ov[q // 2][:, j0:j0 + 4, :], in_=o[:])
+
+        def st_relu_last(pr):
+            if pr // 2 != NQUAD - 1:
+                return
+            o = S[("o", pr // 2)]
+            j1 = (pr % 2) * 2
+            nc.scalar.activation(out=o[:, j1:j1 + 2, :], in_=o[:, j1:j1 + 2, :], func=ACT.Relu)
+            nc.sync.dma_start(out=ov[pr // 4][:, 4 + j1:4 + j1 + 2, :], in_=o[:, j1:j1 + 2, :])
 
         def on(fn, pr):
             if 0 <= pr < NPAIR:
@@ -274,26 +286,33 @@ def tile_l1regressionmoeactionhead_pc_t_kernel(tc, h_attn, x, W_o, b_o, W_ffn, b
             if m % 2 == 0 and 0 <= m // 2 < NQUAD:
                 fn(m // 2)
 
-        for n in range(NPAIR + 20):
-            if n % 4 == 1 and n >= 5 and n // 4 + 2 < NCH:
+        for n in range(NPAIR + 22):
+            if n % 4 == 3 and n >= 7 and n // 4 + 2 < NCH:
                 load_h(n // 4 + 2, 1)
                 load_x(n // 4 + 2, 1)
-            onq(st_recip, n - 9)
-            onq(st_xp, n - 2)
-            onq(st_qx, n - 14)
-            on(st_c, n - 5)
-            on(st_mx1, n - 4)
-            onq(st_qh, n - 3)
-            on(st_h1, n - 16)
-            on(st_mx2, n - 15)
-            onq(st_negmu, n - 6)
-            onq(st_nmr, n - 9)
-            on(st_e, n - 10)
+            if n == 2:
+                prep_wf_transposes()
+            if n == 3:
+                st_xp(2)
+            if n == 5:
+                prep_wf_quantise()
+            if n >= 10:
+                onq(st_xp, n - 4)
+            onq(st_qx, n - 16)
+            on(st_c, n - 7)
+            on(st_mx1, n - 6)
+            onq(st_qh, n - 5)
+            on(st_h1, n - 18)
+            on(st_mx2, n - 17)
+            onq(st_negmu, n - 8)
+            on(st_e, n - 11)
             on(st_a, n - 1)
             on(st_th, n)
-            on(st_d, n - 7)
-            on(st_f, n - 11)
-            on(st_tz, n - 10)
-            onq(st_sqrt, n - 8)
-            onq(st_f2, n - 13)
-            onq(st_relu, n - 19)
+            on(st_d, n - 9)
+            on(st_f, n - 12)
+            on(st_tz, n - 11)
+            onq(st_ars, n - 10)
+            onq(st_nmr, n - 10)
+            onq(st_f2, n - 15)
+            on(st_relu_last, n - 19)
+            onq(st_relu, n - 21)

@@ -167,7 +167,7 @@ def tile_l1regressionmoeactionhead_pc_t_kernel(tc, h_attn, x, W_o, b_o, W_ffn, b
             sums = S[("sums", q)]
             for jj in range(2):
                 j = (pr % 2) * 2 + jj
-                y = work.tile([P, DIM], F32, tag="y", bufs=14, name="y")
+                y = work.tile([P, DIM], F32, tag="y", bufs=16, name="y")
                 S[("y", pr, jj)] = y
                 nc.vector.scalar_tensor_tensor(out=y[:], in0=S[("p1", pr, jj)][:], scalar=0.0, in1=S[("xp", q)][:, j, :],
                                                op0=ALU.add, op1=ALU.add, accum_out=sums[:, j:j + 1])
@@ -264,7 +264,7 @@ def tile_l1regressionmoeactionhead_pc_t_kernel(tc, h_attn, x, W_o, b_o, W_ffn, b
             j0 = (q % 2) * 4
             if q == NQUAD - 1:
                 return
-            if q % 4 == 1:
+            if q % 2 == 1:
                 nc.vector.tensor_scalar(out=o[:], in0=o[:], scalar1=0.0, scalar2=None, op0=ALU.max)
             else:
                 nc.scalar.activation(out=o[:], in_=o[:], func=ACT.Relu)
@@ -286,7 +286,7 @@ def tile_l1regressionmoeactionhead_pc_t_kernel(tc, h_attn, x, W_o, b_o, W_ffn, b
             if m % 2 == 0 and 0 <= m // 2 < NQUAD:
                 fn(m // 2)
 
-        for n in range(NPAIR + 22):
+        for n in range(NPAIR + 24):
             if n % 4 == 3 and n >= 7 and n // 4 + 2 < NCH:
                 load_h(n // 4 + 2, 1)
                 load_x(n // 4 + 2, 1)
@@ -298,21 +298,21 @@ def tile_l1regressionmoeactionhead_pc_t_kernel(tc, h_attn, x, W_o, b_o, W_ffn, b
                 prep_wf_quantise()
             if n >= 10:
                 onq(st_xp, n - 4)
-            onq(st_qx, n - 16)
+            onq(st_qx, n - 18)
             on(st_c, n - 7)
             on(st_mx1, n - 6)
             onq(st_qh, n - 5)
-            on(st_h1, n - 18)
-            on(st_mx2, n - 17)
+            on(st_h1, n - 20)
+            on(st_mx2, n - 19)
             onq(st_negmu, n - 8)
-            on(st_e, n - 11)
+            on(st_e, n - 13)
             on(st_a, n - 1)
             on(st_th, n)
-            on(st_d, n - 9)
-            on(st_f, n - 12)
-            on(st_tz, n - 11)
-            onq(st_ars, n - 10)
-            onq(st_nmr, n - 10)
-            onq(st_f2, n - 15)
-            on(st_relu_last, n - 19)
-            onq(st_relu, n - 21)
+            on(st_d, n - 10)
+            on(st_f, n - 14)
+            on(st_tz, n - 13)
+            onq(st_ars, n - 11)
+            onq(st_nmr, n - 11)
+            onq(st_f2, n - 17)
+            on(st_relu_last, n - 21)
+            onq(st_relu, n - 23)

@@ -20,7 +20,7 @@ NPAIR = TOKENS // (2 * P)
 EPS = 1e-5
 FLOPS = 2 * 2 * TOKENS * DIM * DIM
 
-MANUAL = True
+MANUAL = False
 NQUAD = NPAIR // 2
 
 

@@ -58,20 +58,30 @@ def tile_l1regressionmoeactionhead_pc_t_kernel(tc, h_attn, x, W_o, b_o, W_ffn, b
 
         bo_b = const.tile([P, DIM], BF16)
         nc.scalar.dma_start(out=bo_b[:], in_=b_o.partition_broadcast(P))
-        load_x(0, 2)
+        def load_part(tiles, view, tag, c, j0, j1):
+            if j0 == 0:
+                fresh = loads.tile([P, CH, DIM], BF16, tag=tag, name="ld_" + tag)
+                tiles[c] = fresh
+            nc.sync.dma_start(out=tiles[c][:, j0:j1, :], in_=view[c][:, j0:j1, :])
+
+        load_part(x_tiles, xv, "x", 0, 0, 4)
         wo_sb = const.tile([P, 4, DIM], BF16)
         nc.sync.dma_start(out=wo_sb[:], in_=W_o.rearrange("(r p) k -> p r k", p=P))
-        load_h(0, 4)
+        load_part(h_tiles, hv, "h", 0, 0, 2)
+        load_part(h_tiles, hv, "h", 0, 2, 4)
+        load_part(x_tiles, xv, "x", 0, 4, 8)
+        load_part(h_tiles, hv, "h", 0, 4, 8)
+        load_part(x_tiles, xv, "x", 1, 0, 4)
         gbr = const.tile([P, P], BF16)
         nc.vector.memset(gbr[:], 0.0)
         nc.scalar.dma_start(out=gbr[0:4, :], in_=gamma.rearrange("(t p) -> t p", p=P))
         nc.scalar.dma_start(out=gbr[4:8, :], in_=beta.rearrange("(t p) -> t p", p=P))
         wf_sb = const.tile([P, 4, DIM], BF16)
         nc.sync.dma_start(out=wf_sb[:], in_=W_ffn.rearrange("(r p) k -> p r k", p=P))
-        load_x(1, 2)
         bf_b = const.tile([P, DIM], BF16)
         nc.scalar.dma_start(out=bf_b[:], in_=b_ffn.partition_broadcast(P))
-        load_h(1, 1)
+        load_part(h_tiles, hv, "h", 1, 0, 8)
+        load_part(x_tiles, xv, "x", 1, 4, 8)
         load_h(2, 1)
         load_x(2, 1)
 
@@ -167,7 +177,7 @@ def tile_l1regressionmoeactionhead_pc_t_kernel(tc, h_attn, x, W_o, b_o, W_ffn, b
             sums = S[("sums", q)]
             for jj in range(2):
                 j = (pr % 2) * 2 + jj
-                y = work.tile([P, DIM], F32, tag="y", bufs=16, name="y")
+                y = work.tile([P, DIM], F32, tag="y", bufs=20, name="y")
                 S[("y", pr, jj)] = y
                 nc.vector.scalar_tensor_tensor(out=y[:], in0=S[("p1", pr, jj)][:], scalar=0.0, in1=S[("xp", q)][:, j, :],
                                                op0=ALU.add, op1=ALU.add, accum_out=sums[:, j:j + 1])
@@ -207,27 +217,25 @@ def tile_l1regressionmoeactionhead_pc_t_kernel(tc, h_attn, x, W_o, b_o, W_ffn, b
                 y = S[("y", pr, jj)]
                 nc.scalar.activation(out=y[:], in_=y[:], func=ACT.Identity, bias=S[("nmr", q)][:, j:j + 1], scale=S[("rstd", q)][:, j:j + 1])
 
-        def st_tz(pr):
-            for b in range(2):
-                zt = psum.tile([P, 2, 2, P], F32, tag="zt", name="zt")
-                S[("zt", pr, b)] = zt
-                for tt in range(2):
-                    t = 2 * b + tt
-                    for jj in range(2):
-                        nc.tensor.transpose(zt[:, tt, jj, :], S[("y", pr, jj)][:, t * P:(t + 1) * P], ident_f[:])
+        def st_tz(s):
+            q = s // 2
+            for tt in range(2):
+                t = 2 * (s % 2) + tt
+                zt = psum.tile([P, 4, P], F32, tag="zt", name="zt")
+                S[("zt", q, t)] = zt
+                for j in range(4):
+                    nc.tensor.transpose(zt[:, j, :], S[("y", 2 * q + j // 2, j % 2)][:, t * P:(t + 1) * P], ident_f[:])
 
-        def st_f(pr):
-            q = pr // 2
-            if pr % 2 == 0:
+        def st_f(s):
+            q = s // 2
+            if s % 2 == 0:
                 planes_new = work.tile([P, 4, 4 * P], BF16, tag="planes", bufs=3, name="planes")
                 S[("planes", q)] = planes_new
             planes = S[("planes", q)]
-            c0 = (pr % 2) * 2 * P
-            for b in range(2):
-                for tt in range(2):
-                    t = 2 * b + tt
-                    nc.scalar.activation(out=planes[:, t, c0:c0 + 2 * P], in_=S[("zt", pr, b)][:, tt, :, :].rearrange("p j r -> p (j r)"),
-                                         func=ACT.Identity, bias=gb[:, 4 + t:5 + t], scale=gb[:, t:t + 1])
+            for tt in range(2):
+                t = 2 * (s % 2) + tt
+                nc.scalar.activation(out=planes[:, t, :], in_=S[("zt", q, t)][:].rearrange("p j r -> p (j r)"),
+                                     func=ACT.Identity, bias=gb[:, 4 + t:5 + t], scale=gb[:, t:t + 1])
 
         def st_f2(q):
             xg = work.tile([P, 4 * P, 4], BF16, tag="xg", bufs=2, align_bytes=64, name="xg")
@@ -275,8 +283,14 @@ def tile_l1regressionmoeactionhead_pc_t_kernel(tc, h_attn, x, W_o, b_o, W_ffn, b
                 return
             o = S[("o", pr // 2)]
             j1 = (pr % 2) * 2
-            nc.scalar.activation(out=o[:, j1:j1 + 2, :], in_=o[:, j1:j1 + 2, :], func=ACT.Relu)
-            nc.sync.dma_start(out=ov[pr // 4][:, 4 + j1:4 + j1 + 2, :], in_=o[:, j1:j1 + 2, :])
+            if pr % 2 == 0:
+                nc.scalar.activation(out=o[:, j1:j1 + 2, :], in_=o[:, j1:j1 + 2, :], func=ACT.Relu)
+                nc.sync.dma_start(out=ov[pr // 4][:, 4 + j1:4 + j1 + 2, :], in_=o[:, j1:j1 + 2, :])
+            else:
+                nc.scalar.activation(out=o[:, 2, :], in_=o[:, 2, :], func=ACT.Relu)
+                nc.sync.dma_start(out=ov[pr // 4][:, 6, :], in_=o[:, 2, :])
+                nc.vector.tensor_scalar(out=o[:, 3, :], in0=o[:, 3, :], scalar1=0.0, scalar2=None, op0=ALU.max)
+                nc.sync.dma_start(out=ov[pr // 4][:, 7, :], in_=o[:, 3, :])
 
         def on(fn, pr):
             if 0 <= pr < NPAIR:
@@ -286,7 +300,7 @@ def tile_l1regressionmoeactionhead_pc_t_kernel(tc, h_attn, x, W_o, b_o, W_ffn, b
             if m % 2 == 0 and 0 <= m // 2 < NQUAD:
                 fn(m // 2)
 
-        for n in range(NPAIR + 24):
+        for n in range(NPAIR + 26):
             if n % 4 == 3 and n >= 7 and n // 4 + 2 < NCH:
                 load_h(n // 4 + 2, 1)
                 load_x(n // 4 + 2, 1)
@@ -298,21 +312,21 @@ def tile_l1regressionmoeactionhead_pc_t_kernel(tc, h_attn, x, W_o, b_o, W_ffn, b
                 prep_wf_quantise()
             if n >= 10:
                 onq(st_xp, n - 4)
-            onq(st_qx, n - 18)
+            onq(st_qx, n - 20)
             on(st_c, n - 7)
             on(st_mx1, n - 6)
             onq(st_qh, n - 5)
-            on(st_h1, n - 20)
-            on(st_mx2, n - 19)
+            on(st_h1, n - 22)
+            on(st_mx2, n - 21)
             onq(st_negmu, n - 8)
             on(st_e, n - 13)
             on(st_a, n - 1)
             on(st_th, n)
             on(st_d, n - 10)
-            on(st_f, n - 14)
-            on(st_tz, n - 13)
+            on(st_f, n - 15)
+            on(st_tz, n - 14)
             onq(st_ars, n - 11)
             onq(st_nmr, n - 11)
-            onq(st_f2, n - 17)
-            on(st_relu_last, n - 21)
-            onq(st_relu, n - 23)
+            onq(st_f2, n - 19)
+            on(st_relu_last, n - 23)
+            onq(st_relu, n - 25)

from contextlib import ExitStack

import concourse.mybir as mybir
from concourse.masks import make_identity

F32 = mybir.dt.float32
BF16 = mybir.dt.bfloat16
U32 = mybir.dt.uint32
U8 = mybir.dt.uint8
FP8X4 = mybir.dt.float8_e4m3fn_x4
ALU = mybir.AluOpType
ACT = mybir.ActivationFunctionType

P = 128
DIM = 512
TOKENS = 16 * 512
CH = 8
NCH = TOKENS // (P * CH)
NPAIR = TOKENS // (2 * P)
EPS = 1e-5
FLOPS = 2 * 2 * TOKENS * DIM * DIM

MANUAL = False
NQUAD = NPAIR // 2


def tile_l1regressionmoeactionhead_pc_t_kernel(tc, h_attn, x, W_o, b_o, W_ffn, b_ffn, gamma, beta, out):
    nc = tc.nc
    hv = h_attn.flatten_outer_dims().rearrange("(c p j) k -> c p j k", p=P, j=CH)
    xv = x.flatten_outer_dims().rearrange("(c p j) k -> c p j k", p=P, j=CH)
    ov = out.flatten_outer_dims().rearrange("(c p j) k -> c p j k", p=P, j=CH)

    with ExitStack() as ctx:
        const = ctx.enter_context(tc.tile_pool(name="const", bufs=1))
        loads = ctx.enter_context(tc.tile_pool(name="loads", bufs=3))
        work = ctx.enter_context(tc.tile_pool(name="work", bufs=2))
        stats = ctx.enter_context(tc.tile_pool(name="stats", bufs=4))
        psum = ctx.enter_context(tc.psum_pool(name="psum", bufs=2))
        if MANUAL:
            ctx.enter_context(tc.manual_schedule())

        h_tiles = {}
        x_tiles = {}

        def load_h(c, pieces):
            h_sb = loads.tile([P, CH, DIM], BF16, tag="h", name="h_sb")
            h_tiles[c] = h_sb
            step = CH // pieces
            for i in range(pieces):
                nc.sync.dma_start(out=h_sb[:, i * step:(i + 1) * step, :], in_=hv[c][:, i * step:(i + 1) * step, :])

        def load_x(c, pieces):
            x_sb = loads.tile([P, CH, DIM], BF16, tag="x", name="x_sb")
            x_tiles[c] = x_sb
            step = CH // pieces
            for i in range(pieces):
                nc.sync.dma_start(out=x_sb[:, i * step:(i + 1) * step, :], in_=xv[c][:, i * step:(i + 1) * step, :])

        bo_b = const.tile([P, DIM], BF16)
        nc.scalar.dma_start(out=bo_b[:], in_=b_o.partition_broadcast(P))
        def load_part(tiles, view, tag, c, j0, j1):
            if j0 == 0:
                fresh = loads.tile([P, CH, DIM], BF16, tag=tag, name="ld_" + tag)
                tiles[c] = fresh
            nc.sync.dma_start(out=tiles[c][:, j0:j1, :], in_=view[c][:, j0:j1, :])

        load_part(x_tiles, xv, "x", 0, 0, 4)
        wo_sb = const.tile([P, 4, DIM], BF16)
        nc.sync.dma_start(out=wo_sb[:], in_=W_o.rearrange("(r p) k -> p r k", p=P))
        load_part(h_tiles, hv, "h", 0, 0, 2)
        load_part(h_tiles, hv, "h", 0, 2, 4)
        load_part(x_tiles, xv, "x", 0, 4, 8)
        load_part(h_tiles, hv, "h", 0, 4, 8)
        load_part(x_tiles, xv, "x", 1, 0, 4)
        gbr = const.tile([P, P], BF16)
        nc.vector.memset(gbr[:], 0.0)
        nc.scalar.dma_start(out=gbr[0:4, :], in_=gamma.rearrange("(t p) -> t p", p=P))
        nc.scalar.dma_start(out=gbr[4:8, :], in_=beta.rearrange("(t p) -> t p", p=P))
        wf_sb = const.tile([P, 4, DIM], BF16)
        nc.sync.dma_start(out=wf_sb[:], in_=W_ffn.rearrange("(r p) k -> p r k", p=P))
        bf_b = const.tile([P, DIM], BF16)
        nc.scalar.dma_start(out=bf_b[:], in_=b_ffn.partition_broadcast(P))
        load_part(h_tiles, hv, "h", 1, 0, 8)
        load_part(x_tiles, xv, "x", 1, 4, 8)
        load_h(2, 1)
        load_x(2, 1)

        ident_f = const.tile([P, P], F32)
        make_identity(nc, ident_f[:])
        ident_b = const.tile([P, P], BF16)
        make_identity(nc, ident_b[:])
        eps_t = const.tile([P, 1], F32)
        nc.vector.memset(eps_t[:], EPS)
        warm = const.tile([P, 1], F32)
        nc.scalar.activation(out=warm[:], in_=eps_t[:], func=ACT.Abs_reciprocal_sqrt)

        S = {}

        def st_xp(q):
            xp = work.tile([P, 4, DIM], F32, tag="xp", bufs=3, name="xp")
            S[("xp", q)] = xp
            j0 = (q % 2) * 4
            nc.vector.tensor_tensor(out=xp[:], in0=x_tiles[q // 2][:, j0:j0 + 4, :], in1=bo_b[:].unsqueeze(1).to_broadcast([P, 4, DIM]), op=ALU.add)

        st_xp(0)

        wog = const.tile([P, DIM * 4], BF16, align_bytes=64)
        woc = const.tile([P, DIM], U32, align_bytes=64)
        wos = const.tile([P, DIM], U8, align_bytes=64)
        wog_w = wog[:].bitcast(F32).rearrange("p (r c u) -> p r c u", r=4, u=2)
        for half in range(2):
            wt = psum.tile([P, 2, 2, P], F32, tag="ht", name="wt")
            for rr in range(2):
                for u in range(2):
                    nc.tensor.transpose(wt[:, rr, u, :], wo_sb[:, 2 * half + rr, :].bitcast(F32)[:, u * P:(u + 1) * P], ident_f[:])
            nc.scalar.copy(out=wog_w[:, 2 * half:2 * half + 2, :, :], in_=wt[:].rearrange("p j u r -> p j r u"))
        nc.vector.quantize_mx(out=woc[:].bitcast(FP8X4), scales=wos[:], in_=wog[:])
        st_xp(1)

        gb = const.tile([P, 8], F32)
        wfg = const.tile([P, DIM, 4], BF16, align_bytes=64)
        wfc = const.tile([P, DIM], U32, align_bytes=64)
        wfs = const.tile([P, DIM], U8, align_bytes=64)

        def prep_wf_transposes():
            gb_ps = psum.tile([P, P], BF16, tag="zt", name="gb_ps")
            S["gb_ps"] = gb_ps
            nc.tensor.transpose(gb_ps[:], gbr[:], ident_b[:])
            for r in range(4):
                wt2 = psum.tile([P, 4, P], BF16, tag="p2", name="wt2")
                for t in range(4):
                    nc.tensor.transpose(wt2[:, t, :], wf_sb[:, r, t * P:(t + 1) * P], ident_b[:])
                nc.scalar.copy(out=wfg[:, r * P:(r + 1) * P, :], in_=wt2[:].rearrange("p t c -> p c t"))

        def prep_wf_quantise():
            nc.vector.tensor_copy(out=gb[:], in_=S["gb_ps"][:, 0:8])
            nc.vector.quantize_mx(out=wfc[:].bitcast(FP8X4), scales=wfs[:], in_=wfg[:].rearrange("p c t -> p (c t)"))

        def st_th(pr):
            ht = psum.tile([P, 2, 2, P], F32, tag="ht", name="ht")
            S[("ht", pr)] = ht
            for jj in range(2):
                hsrc = h_tiles[pr // 4][:, (pr % 4) * 2 + jj, :]
                for u in range(2):
                    nc.tensor.transpose(ht[:, jj, u, :], hsrc.bitcast(F32)[:, u * P:(u + 1) * P], ident_f[:])

        def st_a(pr):
            q = pr // 2
            if pr % 2 == 0:
                hg_new = work.tile([P, 4 * DIM], BF16, tag="hg", bufs=4, align_bytes=64, name="hg")
                S[("hg", q)] = hg_new
            hg = S[("hg", q)]
            j0 = (pr % 2) * 2
            nc.scalar.copy(out=hg[:].bitcast(F32).rearrange("p (j r u) -> p j r u", j=4, u=2)[:, j0:j0 + 2, :, :],
                           in_=S[("ht", pr)][:].rearrange("p j u r -> p j r u"))

        def st_qh(q):
            hc = work.tile([P, 4 * P], U32, tag="hc", bufs=3, align_bytes=64, name="hc")
            hs = work.tile([P, 4 * P], U8, tag="hs", bufs=3, align_bytes=64, name="hs")
            S[("hc", q)] = (hc, hs)
            nc.vector.quantize_mx(out=hc[:].bitcast(FP8X4), scales=hs[:], in_=S[("hg", q)][:])

        def st_mx1(pr):
            hc, hs = S[("hc", pr // 2)]
            for jj in range(2):
                c0 = ((pr % 2) * 2 + jj) * P
                p1 = psum.tile([P, DIM], F32, tag="p1", name="p1")
                S[("p1", pr, jj)] = p1
                nc.tensor.matmul_mx(out=p1[:], lhsT=hc[:, c0:c0 + P].bitcast(FP8X4), lhsT_scale=hs[:, c0:c0 + P],
                                    rhs=woc[:].bitcast(FP8X4), rhs_scale=wos[:], start=True, stop=True)

        def st_c(pr):
            q = pr // 2
            if pr % 2 == 0:
                sums_new = stats.tile([P, 4], F32, tag="sums", name="sums")
                S[("sums", q)] = sums_new
            sums = S[("sums", q)]
            for jj in range(2):
                j = (pr % 2) * 2 + jj
                y = work.tile([P, DIM], F32, tag="y", bufs=20, name="y")
                S[("y", pr, jj)] = y
                nc.vector.scalar_tensor_tensor(out=y[:], in0=S[("p1", pr, jj)][:], scalar=0.0, in1=S[("xp", q)][:, j, :],
                                               op0=ALU.add, op1=ALU.add, accum_out=sums[:, j:j + 1])

        def st_negmu(q):
            negmu = stats.tile([P, 4], F32, tag="negmu", name="negmu")
            S[("negmu", q)] = negmu
            nc.gpsimd.tensor_scalar(out=negmu[:], in0=S[("sums", q)][:], scalar1=-1.0 / DIM, scalar2=0.0, op0=ALU.mult, op1=ALU.add)

        def st_d(pr):
            q = pr // 2
            if pr % 2 == 0:
                ssq_new = stats.tile([P, 4], F32, tag="ssq", name="ssq")
                S[("ssq", q)] = ssq_new
            ssq = S[("ssq", q)]
            negmu = S[("negmu", q)]
            for jj in range(2):
                j = (pr % 2) * 2 + jj
                junk = work.tile([P, DIM], BF16, tag="junk", name="junk")
                nc.scalar.activation(out=junk[:], in_=S[("y", pr, jj)][:], func=ACT.Square, bias=negmu[:, j:j + 1], scale=1.0,
                                     accum_out=ssq[:, j:j + 1])

        def st_ars(q):
            rstd = stats.tile([P, 4], F32, tag="rstd", name="rstd")
            S[("rstd", q)] = rstd
            nc.scalar.activation(out=rstd[:], in_=S[("ssq", q)][:], func=ACT.Abs_reciprocal_sqrt, bias=eps_t[:, 0:1], scale=1.0 / DIM)

        def st_nmr(q):
            nmr = stats.tile([P, 4], F32, tag="nmr", name="nmr")
            S[("nmr", q)] = nmr
            nc.gpsimd.tensor_tensor(out=nmr[:], in0=S[("negmu", q)][:], in1=S[("rstd", q)][:], op=ALU.mult)

        def st_e(pr):
            q = pr // 2
            for jj in range(2):
                j = (pr % 2) * 2 + jj
                y = S[("y", pr, jj)]
                nc.scalar.activation(out=y[:], in_=y[:], func=ACT.Identity, bias=S[("nmr", q)][:, j:j + 1], scale=S[("rstd", q)][:, j:j + 1])

        def st_tz(s):
            q = s // 2
            for tt in range(2):
                t = 2 * (s % 2) + tt
                zt = psum.tile([P, 4, P], F32, tag="zt", name="zt")
                S[("zt", q, t)] = zt
                for j in range(4):
                    nc.tensor.transpose(zt[:, j, :], S[("y", 2 * q + j // 2, j % 2)][:, t * P:(t + 1) * P], ident_f[:])

        def st_f(s):
            q = s // 2
            if s % 2 == 0:
                planes_new = work.tile([P, 4, 4 * P], BF16, tag="planes", bufs=3, name="planes")
                S[("planes", q)] = planes_new
            planes = S[("planes", q)]
            for tt in range(2):
                t = 2 * (s % 2) + tt
                nc.scalar.activation(out=planes[:, t, :], in_=S[("zt", q, t)][:].rearrange("p j r -> p (j r)"),
                                     func=ACT.Identity, bias=gb[:, 4 + t:5 + t], scale=gb[:, t:t + 1])

        def st_f2(q):
            xg = work.tile([P, 4 * P, 4], BF16, tag="xg", bufs=2, align_bytes=64, name="xg")
            S[("xg", q)] = xg
            nc.vector.tensor_copy(out=xg[:].rearrange("p (c i) t -> p c t i", i=4),
                                  in_=S[("planes", q)][:].rearrange("p t (c i) -> p c t i", i=4))

        def st_qx(q):
            xc = work.tile([P, 4 * P], U32, tag="xc", bufs=3, align_bytes=64, name="xc")
            xs = work.tile([P, 4 * P], U8, tag="xs", bufs=3, align_bytes=64, name="xs")
            S[("xc", q)] = (xc, xs)
            nc.vector.quantize_mx(out=xc[:].bitcast(FP8X4), scales=xs[:], in_=S[("xg", q)][:].rearrange("p c t -> p (c t)"))

        def st_mx2(pr):
            xc, xs = S[("xc", pr // 2)]
            for jj in range(2):
                c0 = ((pr % 2) * 2 + jj) * P
                p2 = psum.tile([P, DIM], F32, tag="p2", name="p2")
                S[("p2", pr, jj)] = p2
                nc.tensor.matmul_mx(out=p2[:], lhsT=xc[:, c0:c0 + P].bitcast(FP8X4), lhsT_scale=xs[:, c0:c0 + P],
                                    rhs=wfc[:].bitcast(FP8X4), rhs_scale=wfs[:], start=True, stop=True)

        def st_h1(pr):
            q = pr // 2
            if pr % 2 == 0:
                o_new = work.tile([P, 4, DIM], F32, tag="o", bufs=3, name="o")
                S[("o", q)] = o_new
            o = S[("o", q)]
            for jj in range(2):
                nc.vector.tensor_tensor(out=o[:, (pr % 2) * 2 + jj, :], in0=S[("p2", pr, jj)][:], in1=bf_b[:], op=ALU.add)

        def st_relu(q):
            o = S[("o", q)]
            j0 = (q % 2) * 4
            if q == NQUAD - 1:
                return
            if q % 2 == 1:
                nc.vector.tensor_scalar(out=o[:], in0=o[:], scalar1=0.0, scalar2=None, op0=ALU.max)
            else:
                nc.scalar.activation(out=o[:], in_=o[:], func=ACT.Relu)
            nc.sync.dma_start(out=ov[q // 2][:, j0:j0 + 4, :], in_=o[:])

        def st_relu_last(pr):
            if pr // 2 != NQUAD - 1:
                return
            o = S[("o", pr // 2)]
            j1 = (pr % 2) * 2
            if pr % 2 == 0:
                nc.scalar.activation(out=o[:, j1:j1 + 2, :], in_=o[:, j1:j1 + 2, :], func=ACT.Relu)
                nc.sync.dma_start(out=ov[pr // 4][:, 4 + j1:4 + j1 + 2, :], in_=o[:, j1:j1 + 2, :])
            else:
                nc.scalar.activation(out=o[:, 2, :], in_=o[:, 2, :], func=ACT.Relu)
                nc.sync.dma_start(out=ov[pr // 4][:, 6, :], in_=o[:, 2, :])
                nc.vector.tensor_scalar(out=o[:, 3, :], in0=o[:, 3, :], scalar1=0.0, scalar2=None, op0=ALU.max)
                nc.sync.dma_start(out=ov[pr // 4][:, 7, :], in_=o[:, 3, :])

        def on(fn, pr):
            if 0 <= pr < NPAIR:
                fn(pr)

        def onq(fn, m):
            if m % 2 == 0 and 0 <= m // 2 < NQUAD:
                fn(m // 2)

        for n in range(NPAIR + 26):
            if n % 4 == 3 and n >= 7 and n // 4 + 2 < NCH:
                load_h(n // 4 + 2, 1)
                load_x(n // 4 + 2, 1)
            if n == 2:
                prep_wf_transposes()
            if n == 3:
                st_xp(2)
            if n == 5:
                prep_wf_quantise()
            if n >= 10:
                onq(st_xp, n - 4)
            onq(st_qx, n - 20)
            on(st_c, n - 7)
            on(st_mx1, n - 6)
            onq(st_qh, n - 5)
            on(st_h1, n - 22)
            on(st_mx2, n - 21)
            onq(st_negmu, n - 8)
            on(st_e, n - 13)
            on(st_a, n - 1)
            on(st_th, n)
            on(st_d, n - 10)
            on(st_f, n - 15)
            on(st_tz, n - 14)
            onq(st_ars, n - 11)
            onq(st_nmr, n - 11)
            onq(st_f2, n - 19)
            on(st_relu_last, n - 23)
            onq(st_relu, n - 25)
